import numpy as np
import ml_dtypes

BF16 = ml_dtypes.bfloat16


def bf(x):
    return np.asarray(x, np.float32).astype(BF16)


def f32(x):
    return np.asarray(x, np.float32)


def f64(x):
    return np.asarray(x).astype(np.float64)


def striped(idx):
    return np.tile(idx.reshape(-1, 16).T, (8, 1))


S, K, D, M, N = 4096, 128, 64, 128, 1024
EPS = 1e-6


def sigmoid(v):
    return 1.0 / (1.0 + np.exp(-v))


def setup_inputs():
    table = bf(np.random.standard_normal((K, S)))
    wr = np.random.standard_normal((D, D)) / np.sqrt(D)
    wi = np.random.standard_normal((D, D)) / np.sqrt(D)
    w = bf(np.block([[wr.T, wi.T], [-wi.T, wr.T]]))
    ln_scale = f32(np.tile(1.0 + 0.1 * np.random.standard_normal((D, 1)), (M // D, 1)))
    ln_shift = f32(np.tile(0.1 * np.random.standard_normal((D, 1)), (M // D, 1)))
    focus_mask = f32(np.tile(1.0 + 0.1 * np.random.standard_normal((D, 1)), (M // D, 1)))
    mod_bias = f32(np.tile(-(0.1 + 0.1 * np.abs(np.random.standard_normal((D, 1)))), (M // D, 1)))
    return {"table": table, "w": w, "ln_scale": ln_scale, "ln_shift": ln_shift, "focus_mask": focus_mask, "mod_bias": mod_bias, "offs": striped(np.random.permutation(np.tile(np.arange(S), 2))[:N])}


def reference(table, w, ln_scale, ln_shift, focus_mask, mod_bias, offs):
    idx = offs[:16].T.reshape(-1)
    y = f64(w).T @ f64(table)[:, idx]
    mag = np.sqrt(y * y + np.roll(y, D, axis=0) ** 2) + EPS
    mean = mag[:D].mean(0, keepdims=True)
    var = ((mag[:D] - mean) ** 2).sum(0, keepdims=True) / (D - 1)
    nm = (mag - mean) / np.sqrt(var + EPS) * f64(ln_scale) + f64(ln_shift)
    z = nm * (y / mag) * sigmoid(f64(focus_mask))
    nrm = np.sqrt(z * z + np.roll(z, D, axis=0) ** 2) + EPS
    return z * (np.maximum(nrm + f64(mod_bias), 0.0) / nrm)

@@ -1,0 +1,129 @@
+import concourse.mybir as mybir
+
+BF16, F32, U16 = mybir.dt.bfloat16, mybir.dt.float32, mybir.dt.uint16
+ACT = mybir.ActivationFunctionType
+ALU = mybir.AluOpType
+
+P = 128
+S = 4096
+N = 1024
+D = 64
+PIECE = N // 2
+EPS = 1e-6
+TINY = 1e-30
+CHUNKS = 1
+CH = PIECE // CHUNKS
+
+FLOPS = 2 * P * P * N
+
+
+def tile_ubercrsn_kernel(tc, table, w, ln_scale, ln_shift, focus_mask, mod_bias, offs, out):
+    nc = tc.nc
+    with (
+        tc.tile_pool(name="held", bufs=1) as held,
+        tc.tile_pool(name="work", bufs=CHUNKS) as work,
+        tc.psum_pool(name="products", bufs=1) as products,
+        tc.psum_pool(name="sums", bufs=CHUNKS) as sums,
+    ):
+        offsets = held.tile([P, N // 16], U16, name="offsets")
+        nc.sync.dma_start(offsets[:], offs)
+        words = held.tile([P, S], BF16, name="words")
+        nc.sync.dma_start(words[:], table)
+
+        padded = held.tile([P, 5 * D], BF16, name="padded")
+        for stripe in (0, 2, 4):
+            nc.vector.memset(padded[:, stripe * D : (stripe + 1) * D], 0.0)
+        nc.scalar.dma_start(padded[:, D : 2 * D], w[:, 0:D])
+        nc.scalar.dma_start(padded[:, 3 * D : 4 * D], w[:, D : 2 * D])
+
+        gain = held.tile([P, 1], F32, name="gain")
+        shift = held.tile([P, 1], F32, name="shift")
+        focus = held.tile([P, 1], F32, name="focus")
+        bias = held.tile([P, 1], F32, name="bias")
+        nc.gpsimd.dma_start(focus[:], focus_mask)
+        nc.gpsimd.dma_start(gain[:], ln_scale)
+        nc.gpsimd.dma_start(shift[:], ln_shift)
+        nc.gpsimd.dma_start(bias[:], mod_bias)
+
+        one = held.tile([P, 1], F32, name="one")
+        eps = held.tile([P, 1], F32, name="eps")
+        tiny = held.tile([P, 1], F32, name="tiny")
+        nc.vector.memset(one[:], 1.0)
+        nc.vector.memset(eps[:], EPS)
+        nc.vector.memset(tiny[:], TINY)
+
+        averager = held.tile([P, P], BF16, name="averager")
+        nc.vector.memset(averager[:], 0.0)
+        nc.vector.memset(averager[0:D, 0:D], 1.0 / D)
+        nc.vector.memset(averager[D:P, D:P], 1.0 / D)
+
+        gate = held.tile([P, 1], F32, name="gate")
+        nc.scalar.activation(gate[:], focus[:], ACT.Exp, scale=-1.0)
+        nc.scalar.activation(gate[:], gate[:], ACT.Abs_reciprocal_sqrt, bias=one[:])
+        nc.scalar.activation(gate[:], gate[:], ACT.Square)
+        nc.vector.tensor_mul(gain[:], gain[:], gate[:])
+        nc.vector.tensor_mul(shift[:], shift[:], gate[:])
+
+        first = words[:].indirect(offsets[:, 0 : PIECE // 16])
+        second = words[:].indirect(offsets[:, PIECE // 16 : N // 16])
+        real = products.tile([P, PIECE], F32, name="real")
+        imag = products.tile([P, PIECE], F32, name="imag")
+        nc.tensor.matmul(real[:], padded[:, D : 3 * D], first, start=True, stop=False)
+        nc.tensor.matmul(real[:], padded[:, 0 : 2 * D], second, start=False, stop=True)
+        nc.tensor.matmul(imag[:], padded[:, 3 * D : 5 * D], first, start=True, stop=False)
+        nc.tensor.matmul(imag[:], padded[:, 2 * D : 4 * D], second, start=False, stop=True)
+
+        for c in range(CHUNKS):
+            cols = slice(c * CH, (c + 1) * CH)
+
+            re2 = work.tile([P, CH], F32, name="re2")
+            im2 = work.tile([P, CH], F32, name="im2")
+            r2 = work.tile([P, CH], F32, name="r2")
+            inv_r = work.tile([P, CH], F32, name="inv_r")
+            r_bf = work.tile([P, CH], BF16, name="r_bf")
+            r = work.tile([P, CH], F32, name="r")
+            nc.scalar.activation(re2[:], real[:, cols], ACT.Square)
+            nc.scalar.activation(im2[:], imag[:, cols], ACT.Square)
+            nc.vector.tensor_add(r2[:], re2[:], im2[:])
+            nc.scalar.activation(inv_r[:], r2[:], ACT.Abs_reciprocal_sqrt, bias=tiny[:])
+            nc.vector.tensor_mul(r_bf[:], r2[:], inv_r[:])
+            nc.vector.tensor_mul(r[:], r2[:], inv_r[:])
+
+            mean = sums.tile([P, CH], F32, name="mean")
+            nc.tensor.matmul(mean[:], averager[:], r_bf[:], start=True, stop=True)
+            dev = work.tile([P, CH], F32, name="dev")
+            nc.vector.tensor_sub(dev[:], r[:], mean[:])
+            dev2 = work.tile([P, CH], BF16, name="dev2")
+            nc.scalar.activation(dev2[:], dev[:], ACT.Square)
+            mean_dev2 = sums.tile([P, CH], F32, name="mean_dev2")
+            nc.tensor.matmul(mean_dev2[:], averager[:], dev2[:], start=True, stop=True)
+            rstd = work.tile([P, CH], F32, name="rstd")
+            nc.scalar.activation(rstd[:], mean_dev2[:], ACT.Abs_reciprocal_sqrt, bias=eps[:], scale=D / (D - 1.0))
+
+            inv_mag = work.tile([P, CH], F32, name="inv_mag")
+            nc.scalar.activation(inv_mag[:], r[:], ACT.Abs_reciprocal_sqrt, bias=eps[:])
+            nc.scalar.activation(inv_mag[:], inv_mag[:], ACT.Square)
+
+            factor = work.tile([P, CH], F32, name="factor")
+            nc.vector.scalar_tensor_tensor(factor[:], dev[:], gain[:], rstd[:], ALU.mult, ALU.mult)
+            nc.vector.scalar_tensor_tensor(factor[:], factor[:], shift[:], inv_mag[:], ALU.add, ALU.mult)
+
+            z_abs = work.tile([P, CH], F32, name="z_abs")
+            nc.scalar.activation(z_abs[:], factor[:], ACT.Abs)
+            nc.vector.tensor_mul(z_abs[:], z_abs[:], r[:])
+            keep = work.tile([P, CH], F32, name="keep")
+            nc.scalar.activation(keep[:], z_abs[:], ACT.Abs_reciprocal_sqrt, bias=eps[:])
+            nc.vector.scalar_tensor_tensor(keep[:], keep[:], bias[:], keep[:], ALU.mult, ALU.mult)
+            nc.scalar.activation(keep[:], keep[:], ACT.Relu, bias=one[:])
+            nc.vector.tensor_mul(factor[:], factor[:], keep[:])
+
+            out_re = work.tile([P, CH], F32, name="out_re")
+            out_im = work.tile([P, CH], F32, name="out_im")
+            nc.vector.tensor_mul(out_re[:], real[:, cols], factor[:])
+            nc.vector.tensor_mul(out_im[:], imag[:, cols], factor[:])
+
+            for half in range(2):
+                rows = slice(half * D, (half + 1) * D)
+                to = slice(half * PIECE + c * CH, half * PIECE + (c + 1) * CH)
+                nc.sync.dma_start(out[0:D, to], out_re[rows, :])
+                nc.scalar.dma_start(out[D:P, to], out_im[rows, :])

@@ -11,7 +11,7 @@ D = 64
 PIECE = N // 2
 EPS = 1e-6
 TINY = 1e-30
-CHUNKS = 1
+CHUNKS = 2
 CH = PIECE // CHUNKS
 
 FLOPS = 2 * P * P * N
@@ -36,14 +36,14 @@ def tile_ubercrsn_kernel(tc, table, w, ln_scale, ln_shift, focus_mask, mod_bias,
         nc.scalar.dma_start(padded[:, D : 2 * D], w[:, 0:D])
         nc.scalar.dma_start(padded[:, 3 * D : 4 * D], w[:, D : 2 * D])
 
-        gain = held.tile([P, 1], F32, name="gain")
-        shift = held.tile([P, 1], F32, name="shift")
         focus = held.tile([P, 1], F32, name="focus")
-        bias = held.tile([P, 1], F32, name="bias")
-        nc.gpsimd.dma_start(focus[:], focus_mask)
-        nc.gpsimd.dma_start(gain[:], ln_scale)
-        nc.gpsimd.dma_start(shift[:], ln_shift)
-        nc.gpsimd.dma_start(bias[:], mod_bias)
+        ln_gain = held.tile([P, 1], F32, name="ln_gain")
+        ln_bias = held.tile([P, 1], F32, name="ln_bias")
+        relu_bias = held.tile([P, 1], F32, name="relu_bias")
+        nc.scalar.dma_start(focus[:], focus_mask)
+        nc.scalar.dma_start(ln_gain[:], ln_scale)
+        nc.scalar.dma_start(ln_bias[:], ln_shift)
+        nc.scalar.dma_start(relu_bias[:], mod_bias)
 
         one = held.tile([P, 1], F32, name="one")
         eps = held.tile([P, 1], F32, name="eps")
@@ -56,13 +56,25 @@ def tile_ubercrsn_kernel(tc, table, w, ln_scale, ln_shift, focus_mask, mod_bias,
         nc.vector.memset(averager[:], 0.0)
         nc.vector.memset(averager[0:D, 0:D], 1.0 / D)
         nc.vector.memset(averager[D:P, D:P], 1.0 / D)
+        centerer = held.tile([P, P], F32, name="centerer")
+        nc.gpsimd.memset(centerer[:], 0.0)
+        nc.gpsimd.memset(centerer[0:D, 0:D], -1.0 / D)
+        nc.gpsimd.memset(centerer[D:P, D:P], -1.0 / D)
+        nc.gpsimd.affine_select(
+            out=centerer[:], in_=centerer[:], compare_op=ALU.not_equal, fill=1.0 - 1.0 / D,
+            base=0, pattern=[[-1, P]], channel_multiplier=1,
+        )
 
+        exp_neg = held.tile([P, 1], F32, name="exp_neg")
+        gate_root = held.tile([P, 1], F32, name="gate_root")
         gate = held.tile([P, 1], F32, name="gate")
-        nc.scalar.activation(gate[:], focus[:], ACT.Exp, scale=-1.0)
-        nc.scalar.activation(gate[:], gate[:], ACT.Abs_reciprocal_sqrt, bias=one[:])
-        nc.scalar.activation(gate[:], gate[:], ACT.Square)
-        nc.vector.tensor_mul(gain[:], gain[:], gate[:])
-        nc.vector.tensor_mul(shift[:], shift[:], gate[:])
+        nc.scalar.activation(exp_neg[:], focus[:], ACT.Exp, scale=-1.0)
+        nc.scalar.activation(gate_root[:], exp_neg[:], ACT.Abs_reciprocal_sqrt, bias=one[:])
+        nc.scalar.activation(gate[:], gate_root[:], ACT.Square)
+        gain = held.tile([P, 1], F32, name="gain")
+        shift = held.tile([P, 1], F32, name="shift")
+        nc.vector.tensor_mul(gain[:], ln_gain[:], gate[:])
+        nc.vector.tensor_mul(shift[:], ln_bias[:], gate[:])
 
         first = words[:].indirect(offsets[:, 0 : PIECE // 16])
         second = words[:].indirect(offsets[:, PIECE // 16 : N // 16])
@@ -80,19 +92,15 @@ def tile_ubercrsn_kernel(tc, table, w, ln_scale, ln_shift, focus_mask, mod_bias,
             im2 = work.tile([P, CH], F32, name="im2")
             r2 = work.tile([P, CH], F32, name="r2")
             inv_r = work.tile([P, CH], F32, name="inv_r")
-            r_bf = work.tile([P, CH], BF16, name="r_bf")
             r = work.tile([P, CH], F32, name="r")
             nc.scalar.activation(re2[:], real[:, cols], ACT.Square)
             nc.scalar.activation(im2[:], imag[:, cols], ACT.Square)
             nc.vector.tensor_add(r2[:], re2[:], im2[:])
             nc.scalar.activation(inv_r[:], r2[:], ACT.Abs_reciprocal_sqrt, bias=tiny[:])
-            nc.vector.tensor_mul(r_bf[:], r2[:], inv_r[:])
             nc.vector.tensor_mul(r[:], r2[:], inv_r[:])
 
-            mean = sums.tile([P, CH], F32, name="mean")
-            nc.tensor.matmul(mean[:], averager[:], r_bf[:], start=True, stop=True)
-            dev = work.tile([P, CH], F32, name="dev")
-            nc.vector.tensor_sub(dev[:], r[:], mean[:])
+            dev = sums.tile([P, CH], F32, name="dev")
+            nc.tensor.matmul(dev[:], centerer[:], r[:], start=True, stop=True)
             dev2 = work.tile([P, CH], BF16, name="dev2")
             nc.scalar.activation(dev2[:], dev[:], ACT.Square)
             mean_dev2 = sums.tile([P, CH], F32, name="mean_dev2")
@@ -100,27 +108,37 @@ def tile_ubercrsn_kernel(tc, table, w, ln_scale, ln_shift, focus_mask, mod_bias,
             rstd = work.tile([P, CH], F32, name="rstd")
             nc.scalar.activation(rstd[:], mean_dev2[:], ACT.Abs_reciprocal_sqrt, bias=eps[:], scale=D / (D - 1.0))
 
+            inv_mag_root = work.tile([P, CH], F32, name="inv_mag_root")
             inv_mag = work.tile([P, CH], F32, name="inv_mag")
-            nc.scalar.activation(inv_mag[:], r[:], ACT.Abs_reciprocal_sqrt, bias=eps[:])
-            nc.scalar.activation(inv_mag[:], inv_mag[:], ACT.Square)
+            shrink = work.tile([P, CH], F32, name="shrink")
+            nc.scalar.activation(inv_mag_root[:], r[:], ACT.Abs_reciprocal_sqrt, bias=eps[:])
+            nc.gpsimd.tensor_mul(inv_mag[:], inv_mag_root[:], inv_mag_root[:])
+            nc.gpsimd.tensor_mul(shrink[:], r[:], inv_mag[:])
 
+            scaled = work.tile([P, CH], F32, name="scaled")
             factor = work.tile([P, CH], F32, name="factor")
-            nc.vector.scalar_tensor_tensor(factor[:], dev[:], gain[:], rstd[:], ALU.mult, ALU.mult)
-            nc.vector.scalar_tensor_tensor(factor[:], factor[:], shift[:], inv_mag[:], ALU.add, ALU.mult)
+            gated_abs = work.tile([P, CH], F32, name="gated_abs")
+            nc.vector.scalar_tensor_tensor(scaled[:], dev[:], gain[:], rstd[:], ALU.mult, ALU.mult)
+            nc.scalar.activation(gated_abs[:], scaled[:], ACT.Abs, bias=shift[:])
+            nc.vector.scalar_tensor_tensor(factor[:], scaled[:], shift[:], inv_mag[:], ALU.add, ALU.mult)
 
             z_abs = work.tile([P, CH], F32, name="z_abs")
-            nc.scalar.activation(z_abs[:], factor[:], ACT.Abs)
-            nc.vector.tensor_mul(z_abs[:], z_abs[:], r[:])
+            inv_nrm_root = work.tile([P, CH], F32, name="inv_nrm_root")
+            b_over_nrm = work.tile([P, CH], F32, name="b_over_nrm")
             keep = work.tile([P, CH], F32, name="keep")
-            nc.scalar.activation(keep[:], z_abs[:], ACT.Abs_reciprocal_sqrt, bias=eps[:])
-            nc.vector.scalar_tensor_tensor(keep[:], keep[:], bias[:], keep[:], ALU.mult, ALU.mult)
-            nc.scalar.activation(keep[:], keep[:], ACT.Relu, bias=one[:])
-            nc.vector.tensor_mul(factor[:], factor[:], keep[:])
+            nc.vector.tensor_mul(z_abs[:], gated_abs[:], shrink[:])
+            nc.scalar.activation(inv_nrm_root[:], z_abs[:], ACT.Abs_reciprocal_sqrt, bias=eps[:])
+            nc.vector.scalar_tensor_tensor(
+                b_over_nrm[:], inv_nrm_root[:], relu_bias[:], inv_nrm_root[:], ALU.mult, ALU.mult
+            )
+            nc.scalar.activation(keep[:], b_over_nrm[:], ACT.Relu, bias=one[:])
 
+            kept = work.tile([P, CH], F32, name="kept")
             out_re = work.tile([P, CH], F32, name="out_re")
             out_im = work.tile([P, CH], F32, name="out_im")
-            nc.vector.tensor_mul(out_re[:], real[:, cols], factor[:])
-            nc.vector.tensor_mul(out_im[:], imag[:, cols], factor[:])
+            nc.vector.tensor_mul(kept[:], factor[:], keep[:])
+            nc.vector.tensor_mul(out_re[:], real[:, cols], kept[:])
+            nc.vector.tensor_mul(out_im[:], imag[:, cols], kept[:])
 
             for half in range(2):
                 rows = slice(half * D, (half + 1) * D)

@@ -11,8 +11,9 @@ D = 64
 PIECE = N // 2
 EPS = 1e-6
 TINY = 1e-30
-CHUNKS = 2
+CHUNKS = 4
 CH = PIECE // CHUNKS
+WARM_UPS = 7
 
 FLOPS = 2 * P * P * N
 
@@ -21,35 +22,36 @@ def tile_ubercrsn_kernel(tc, table, w, ln_scale, ln_shift, focus_mask, mod_bias,
     nc = tc.nc
     with (
         tc.tile_pool(name="held", bufs=1) as held,
-        tc.tile_pool(name="work", bufs=CHUNKS) as work,
-        tc.psum_pool(name="products", bufs=1) as products,
-        tc.psum_pool(name="sums", bufs=CHUNKS) as sums,
+        tc.tile_pool(name="work", bufs=1) as work,
+        tc.psum_pool(name="psum", bufs=1) as psum,
     ):
+        focus = held.tile([P, 1], F32, name="focus")
+        nc.sync.dma_start(focus[:], focus_mask)
         offsets = held.tile([P, N // 16], U16, name="offsets")
         nc.sync.dma_start(offsets[:], offs)
         words = held.tile([P, S], BF16, name="words")
-        nc.sync.dma_start(words[:], table)
+        nc.scalar.dma_start(words[:], table)
 
         padded = held.tile([P, 5 * D], BF16, name="padded")
         for stripe in (0, 2, 4):
             nc.vector.memset(padded[:, stripe * D : (stripe + 1) * D], 0.0)
-        nc.scalar.dma_start(padded[:, D : 2 * D], w[:, 0:D])
-        nc.scalar.dma_start(padded[:, 3 * D : 4 * D], w[:, D : 2 * D])
+        nc.sync.dma_start(padded[:, D : 2 * D], w[:, 0:D])
+        nc.sync.dma_start(padded[:, 3 * D : 4 * D], w[:, D : 2 * D])
 
-        focus = held.tile([P, 1], F32, name="focus")
         ln_gain = held.tile([P, 1], F32, name="ln_gain")
         ln_bias = held.tile([P, 1], F32, name="ln_bias")
         relu_bias = held.tile([P, 1], F32, name="relu_bias")
-        nc.scalar.dma_start(focus[:], focus_mask)
-        nc.scalar.dma_start(ln_gain[:], ln_scale)
-        nc.scalar.dma_start(ln_bias[:], ln_shift)
-        nc.scalar.dma_start(relu_bias[:], mod_bias)
+        nc.sync.dma_start(ln_gain[:], ln_scale)
+        nc.sync.dma_start(ln_bias[:], ln_shift)
+        nc.sync.dma_start(relu_bias[:], mod_bias)
 
         one = held.tile([P, 1], F32, name="one")
         eps = held.tile([P, 1], F32, name="eps")
+        eps_squared = held.tile([P, 1], F32, name="eps_squared")
         tiny = held.tile([P, 1], F32, name="tiny")
         nc.vector.memset(one[:], 1.0)
         nc.vector.memset(eps[:], EPS)
+        nc.vector.memset(eps_squared[:], EPS * EPS)
         nc.vector.memset(tiny[:], TINY)
 
         averager = held.tile([P, P], BF16, name="averager")
@@ -65,6 +67,12 @@ def tile_ubercrsn_kernel(tc, table, w, ln_scale, ln_shift, focus_mask, mod_bias,
             base=0, pattern=[[-1, P]], channel_multiplier=1,
         )
 
+        warm_in = held.tile([P, PIECE], BF16, name="warm_in")
+        nc.vector.memset(warm_in[:], 0.0)
+        warm_out = psum.tile([P, PIECE], F32, name="warm_out")
+        for i in range(WARM_UPS):
+            nc.tensor.matmul(warm_out[:], averager[:], warm_in[:], start=True, stop=True)
+
         exp_neg = held.tile([P, 1], F32, name="exp_neg")
         gate_root = held.tile([P, 1], F32, name="gate_root")
         gate = held.tile([P, 1], F32, name="gate")
@@ -78,70 +86,91 @@ def tile_ubercrsn_kernel(tc, table, w, ln_scale, ln_shift, focus_mask, mod_bias,
 
         first = words[:].indirect(offsets[:, 0 : PIECE // 16])
         second = words[:].indirect(offsets[:, PIECE // 16 : N // 16])
-        real = products.tile([P, PIECE], F32, name="real")
-        imag = products.tile([P, PIECE], F32, name="imag")
+        real = psum.tile([P, PIECE], F32, name="real")
+        imag = psum.tile([P, PIECE], F32, name="imag")
         nc.tensor.matmul(real[:], padded[:, D : 3 * D], first, start=True, stop=False)
         nc.tensor.matmul(real[:], padded[:, 0 : 2 * D], second, start=False, stop=True)
         nc.tensor.matmul(imag[:], padded[:, 3 * D : 5 * D], first, start=True, stop=False)
         nc.tensor.matmul(imag[:], padded[:, 2 * D : 4 * D], second, start=False, stop=True)
 
-        for c in range(CHUNKS):
-            cols = slice(c * CH, (c + 1) * CH)
+        chunks = range(CHUNKS)
+        cols = [slice(c * CH, (c + 1) * CH) for c in chunks]
 
-            re2 = work.tile([P, CH], F32, name="re2")
-            im2 = work.tile([P, CH], F32, name="im2")
-            r2 = work.tile([P, CH], F32, name="r2")
-            inv_r = work.tile([P, CH], F32, name="inv_r")
-            r = work.tile([P, CH], F32, name="r")
-            nc.scalar.activation(re2[:], real[:, cols], ACT.Square)
-            nc.scalar.activation(im2[:], imag[:, cols], ACT.Square)
-            nc.vector.tensor_add(r2[:], re2[:], im2[:])
-            nc.scalar.activation(inv_r[:], r2[:], ACT.Abs_reciprocal_sqrt, bias=tiny[:])
-            nc.vector.tensor_mul(r[:], r2[:], inv_r[:])
+        def per_chunk(dtype, name):
+            return [work.tile([P, CH], dtype, name=f"{name}{c}")[:] for c in chunks]
 
-            dev = sums.tile([P, CH], F32, name="dev")
-            nc.tensor.matmul(dev[:], centerer[:], r[:], start=True, stop=True)
-            dev2 = work.tile([P, CH], BF16, name="dev2")
-            nc.scalar.activation(dev2[:], dev[:], ACT.Square)
-            mean_dev2 = sums.tile([P, CH], F32, name="mean_dev2")
-            nc.tensor.matmul(mean_dev2[:], averager[:], dev2[:], start=True, stop=True)
-            rstd = work.tile([P, CH], F32, name="rstd")
-            nc.scalar.activation(rstd[:], mean_dev2[:], ACT.Abs_reciprocal_sqrt, bias=eps[:], scale=D / (D - 1.0))
+        def per_chunk_psum(name):
+            banks = [psum.tile([P, 2 * CH], F32, name=f"{name}{i}") for i in range(CHUNKS // 2)]
+            return [banks[c // 2][:, (c % 2) * CH : (c % 2 + 1) * CH] for c in chunks]
 
-            inv_mag_root = work.tile([P, CH], F32, name="inv_mag_root")
-            inv_mag = work.tile([P, CH], F32, name="inv_mag")
-            shrink = work.tile([P, CH], F32, name="shrink")
-            nc.scalar.activation(inv_mag_root[:], r[:], ACT.Abs_reciprocal_sqrt, bias=eps[:])
-            nc.gpsimd.tensor_mul(inv_mag[:], inv_mag_root[:], inv_mag_root[:])
-            nc.gpsimd.tensor_mul(shrink[:], r[:], inv_mag[:])
+        re2 = per_chunk(F32, "re2")
+        im2 = per_chunk(F32, "im2")
+        r2 = per_chunk(F32, "r2")
+        inv_r = per_chunk(F32, "inv_r")
+        r = per_chunk(F32, "r")
+        for c in chunks:
+            nc.scalar.activation(re2[c], real[:, cols[c]], ACT.Square)
+        for c in chunks:
+            nc.scalar.activation(im2[c], imag[:, cols[c]], ACT.Square)
+        for c in chunks:
+            nc.vector.tensor_add(r2[c], re2[c], im2[c])
+        for c in chunks:
+            nc.scalar.activation(inv_r[c], r2[c], ACT.Abs_reciprocal_sqrt, bias=tiny[:])
+        for c in chunks:
+            nc.vector.tensor_mul(r[c], r2[c], inv_r[c])
 
-            scaled = work.tile([P, CH], F32, name="scaled")
-            factor = work.tile([P, CH], F32, name="factor")
-            gated_abs = work.tile([P, CH], F32, name="gated_abs")
-            nc.vector.scalar_tensor_tensor(scaled[:], dev[:], gain[:], rstd[:], ALU.mult, ALU.mult)
-            nc.scalar.activation(gated_abs[:], scaled[:], ACT.Abs, bias=shift[:])
-            nc.vector.scalar_tensor_tensor(factor[:], scaled[:], shift[:], inv_mag[:], ALU.add, ALU.mult)
+        dev = per_chunk_psum("dev")
+        for c in chunks:
+            nc.tensor.matmul(dev[c], centerer[:], r[c], start=True, stop=True)
 
-            z_abs = work.tile([P, CH], F32, name="z_abs")
-            inv_nrm_root = work.tile([P, CH], F32, name="inv_nrm_root")
-            b_over_nrm = work.tile([P, CH], F32, name="b_over_nrm")
-            keep = work.tile([P, CH], F32, name="keep")
-            nc.vector.tensor_mul(z_abs[:], gated_abs[:], shrink[:])
-            nc.scalar.activation(inv_nrm_root[:], z_abs[:], ACT.Abs_reciprocal_sqrt, bias=eps[:])
+        inv_mag_root = per_chunk(F32, "inv_mag_root")
+        inv_mag = per_chunk(F32, "inv_mag")
+        for c in chunks:
+            nc.scalar.activation(inv_mag_root[c], r[c], ACT.Abs_reciprocal_sqrt, bias=eps[:])
+        for c in chunks:
+            nc.vector.tensor_mul(inv_mag[c], inv_mag_root[c], inv_mag_root[c])
+
+        dev2 = per_chunk(BF16, "dev2")
+        mean_dev2 = per_chunk_psum("mean_dev2")
+        rstd = per_chunk(F32, "rstd")
+        for c in chunks:
+            nc.scalar.activation(dev2[c], dev[c], ACT.Square)
+        for c in chunks:
+            nc.tensor.matmul(mean_dev2[c], averager[:], dev2[c], start=True, stop=True)
+        for c in chunks:
+            nc.scalar.activation(rstd[c], mean_dev2[c], ACT.Abs_reciprocal_sqrt, bias=eps[:], scale=D / (D - 1.0))
+
+        scaled = per_chunk(F32, "scaled")
+        gated_abs = per_chunk(F32, "gated_abs")
+        mag_nrm = per_chunk(F32, "mag_nrm")
+        inv_mag_nrm_root = per_chunk(F32, "inv_mag_nrm_root")
+        inv_mag_nrm = per_chunk(F32, "inv_mag_nrm")
+        keep_over_mag = per_chunk(F32, "keep_over_mag")
+        y_gated = [work.tile([P, 2, CH], F32, name=f"y_gated{c}") for c in chunks]
+        result = [work.tile([P, 2, CH], F32, name=f"result{c}") for c in chunks]
+        for c in chunks:
+            nc.vector.scalar_tensor_tensor(scaled[c], dev[c], gain[:], rstd[c], ALU.mult, ALU.mult)
+        for c in chunks:
+            nc.scalar.activation(gated_abs[c], scaled[c], ACT.Abs, bias=shift[:])
+        for c in chunks:
+            nc.vector.scalar_tensor_tensor(mag_nrm[c], gated_abs[c], EPS, r[c], ALU.add, ALU.mult)
+        for c in chunks:
+            nc.scalar.activation(inv_mag_nrm_root[c], mag_nrm[c], ACT.Abs_reciprocal_sqrt, bias=eps_squared[:])
+        for c in chunks:
+            nc.scalar.activation(inv_mag_nrm[c], inv_mag_nrm_root[c], ACT.Square)
+        for c in chunks:
+            nc.vector.scalar_tensor_tensor(y_gated[c][:, 0, :], scaled[c], shift[:], real[:, cols[c]], ALU.add, ALU.mult)
+            nc.vector.scalar_tensor_tensor(y_gated[c][:, 1, :], scaled[c], shift[:], imag[:, cols[c]], ALU.add, ALU.mult)
+        for c in chunks:
             nc.vector.scalar_tensor_tensor(
-                b_over_nrm[:], inv_nrm_root[:], relu_bias[:], inv_nrm_root[:], ALU.mult, ALU.mult
+                keep_over_mag[c], inv_mag_nrm[c], relu_bias[:], inv_mag[c], ALU.mult, ALU.add
             )
-            nc.scalar.activation(keep[:], b_over_nrm[:], ACT.Relu, bias=one[:])
-
-            kept = work.tile([P, CH], F32, name="kept")
-            out_re = work.tile([P, CH], F32, name="out_re")
-            out_im = work.tile([P, CH], F32, name="out_im")
-            nc.vector.tensor_mul(kept[:], factor[:], keep[:])
-            nc.vector.tensor_mul(out_re[:], real[:, cols], kept[:])
-            nc.vector.tensor_mul(out_im[:], imag[:, cols], kept[:])
-
+        out_by_feature = out.rearrange("(part m) n -> m part n", part=2)
+        for c in chunks:
+            for part in range(2):
+                nc.vector.scalar_tensor_tensor(
+                    result[c][:, part, :], keep_over_mag[c], 0.0, y_gated[c][:, part, :], ALU.max, ALU.mult
+                )
             for half in range(2):
-                rows = slice(half * D, (half + 1) * D)
                 to = slice(half * PIECE + c * CH, half * PIECE + (c + 1) * CH)
-                nc.sync.dma_start(out[0:D, to], out_re[rows, :])
-                nc.scalar.dma_start(out[D:P, to], out_im[rows, :])
+                nc.sync.dma_start(out_by_feature[:, :, to], result[c][half * D : (half + 1) * D, :, :])

@@ -1,3 +1,5 @@
+import math
+
 import concourse.mybir as mybir
 
 BF16, F32, U16 = mybir.dt.bfloat16, mybir.dt.float32, mybir.dt.uint16
@@ -13,7 +15,8 @@ EPS = 1e-6
 TINY = 1e-30
 CHUNKS = 4
 CH = PIECE // CHUNKS
-WARM_UPS = 7
+QUARTER = S // 4
+WARM_UPS = 5
 
 FLOPS = 2 * P * P * N
 
@@ -30,11 +33,12 @@ def tile_ubercrsn_kernel(tc, table, w, ln_scale, ln_shift, focus_mask, mod_bias,
         offsets = held.tile([P, N // 16], U16, name="offsets")
         nc.sync.dma_start(offsets[:], offs)
         words = held.tile([P, S], BF16, name="words")
-        nc.scalar.dma_start(words[:], table)
+        for q in range(4):
+            nc.scalar.dma_start(words[:, q * QUARTER : (q + 1) * QUARTER], table[:, q * QUARTER : (q + 1) * QUARTER])
 
         padded = held.tile([P, 5 * D], BF16, name="padded")
         for stripe in (0, 2, 4):
-            nc.vector.memset(padded[:, stripe * D : (stripe + 1) * D], 0.0)
+            nc.gpsimd.memset(padded[:, stripe * D : (stripe + 1) * D], 0.0)
         nc.sync.dma_start(padded[:, D : 2 * D], w[:, 0:D])
         nc.sync.dma_start(padded[:, 3 * D : 4 * D], w[:, D : 2 * D])
 
@@ -46,39 +50,36 @@ def tile_ubercrsn_kernel(tc, table, w, ln_scale, ln_shift, focus_mask, mod_bias,
         nc.sync.dma_start(relu_bias[:], mod_bias)
 
         one = held.tile([P, 1], F32, name="one")
-        eps = held.tile([P, 1], F32, name="eps")
-        eps_squared = held.tile([P, 1], F32, name="eps_squared")
-        tiny = held.tile([P, 1], F32, name="tiny")
         nc.vector.memset(one[:], 1.0)
-        nc.vector.memset(eps[:], EPS)
-        nc.vector.memset(eps_squared[:], EPS * EPS)
-        nc.vector.memset(tiny[:], TINY)
-
+        first_use = held.tile([P, 1], F32, name="first_use")
+        nc.scalar.activation(first_use[:], one[:], ACT.Abs_reciprocal_sqrt)
         averager = held.tile([P, P], BF16, name="averager")
         nc.vector.memset(averager[:], 0.0)
         nc.vector.memset(averager[0:D, 0:D], 1.0 / D)
         nc.vector.memset(averager[D:P, D:P], 1.0 / D)
-        centerer = held.tile([P, P], F32, name="centerer")
-        nc.gpsimd.memset(centerer[:], 0.0)
-        nc.gpsimd.memset(centerer[0:D, 0:D], -1.0 / D)
-        nc.gpsimd.memset(centerer[D:P, D:P], -1.0 / D)
-        nc.gpsimd.affine_select(
-            out=centerer[:], in_=centerer[:], compare_op=ALU.not_equal, fill=1.0 - 1.0 / D,
-            base=0, pattern=[[-1, P]], channel_multiplier=1,
-        )
+        zeros = held.tile([P, PIECE], BF16, name="zeros")
+        nc.vector.memset(zeros[:], 0.0)
+        eps = held.tile([P, 1], F32, name="eps")
+        eps_squared = held.tile([P, 1], F32, name="eps_squared")
+        tiny = held.tile([P, 1], F32, name="tiny")
+        inv_e = held.tile([P, 1], F32, name="inv_e")
+        nc.vector.memset(eps[:], EPS)
+        nc.vector.memset(eps_squared[:], EPS * EPS)
+        nc.vector.memset(tiny[:], TINY)
+        nc.vector.memset(inv_e[:], math.exp(-1.0))
 
-        warm_in = held.tile([P, PIECE], BF16, name="warm_in")
-        nc.vector.memset(warm_in[:], 0.0)
-        warm_out = psum.tile([P, PIECE], F32, name="warm_out")
+        idle_product = psum.tile([P, PIECE], F32, name="idle_product")
         for i in range(WARM_UPS):
-            nc.tensor.matmul(warm_out[:], averager[:], warm_in[:], start=True, stop=True)
+            nc.tensor.matmul(idle_product[:], averager[:], zeros[:], start=True, stop=True)
+        for q in range(3):
+            nc.tensor.matmul(idle_product[:], averager[:], words[:, q * QUARTER : q * QUARTER + PIECE], start=True, stop=True)
 
         exp_neg = held.tile([P, 1], F32, name="exp_neg")
-        gate_root = held.tile([P, 1], F32, name="gate_root")
+        one_plus_exp = held.tile([P, 1], F32, name="one_plus_exp")
         gate = held.tile([P, 1], F32, name="gate")
-        nc.scalar.activation(exp_neg[:], focus[:], ACT.Exp, scale=-1.0)
-        nc.scalar.activation(gate_root[:], exp_neg[:], ACT.Abs_reciprocal_sqrt, bias=one[:])
-        nc.scalar.activation(gate[:], gate_root[:], ACT.Square)
+        nc.gpsimd.tensor_tensor(exp_neg[:], inv_e[:], focus[:], ALU.pow)
+        nc.vector.tensor_scalar_add(one_plus_exp[:], exp_neg[:], 1.0)
+        nc.vector.reciprocal(gate[:], one_plus_exp[:])
         gain = held.tile([P, 1], F32, name="gain")
         shift = held.tile([P, 1], F32, name="shift")
         nc.vector.tensor_mul(gain[:], ln_gain[:], gate[:])
@@ -107,6 +108,7 @@ def tile_ubercrsn_kernel(tc, table, w, ln_scale, ln_shift, focus_mask, mod_bias,
         im2 = per_chunk(F32, "im2")
         r2 = per_chunk(F32, "r2")
         inv_r = per_chunk(F32, "inv_r")
+        r_bf = per_chunk(BF16, "r_bf")
         r = per_chunk(F32, "r")
         for c in chunks:
             nc.scalar.activation(re2[c], real[:, cols[c]], ACT.Square)
@@ -117,11 +119,16 @@ def tile_ubercrsn_kernel(tc, table, w, ln_scale, ln_shift, focus_mask, mod_bias,
         for c in chunks:
             nc.scalar.activation(inv_r[c], r2[c], ACT.Abs_reciprocal_sqrt, bias=tiny[:])
         for c in chunks:
+            nc.vector.tensor_mul(r_bf[c], r2[c], inv_r[c])
+        for c in chunks:
             nc.vector.tensor_mul(r[c], r2[c], inv_r[c])
 
-        dev = per_chunk_psum("dev")
+        mean = per_chunk_psum("mean")
+        dev = per_chunk(F32, "dev")
         for c in chunks:
-            nc.tensor.matmul(dev[c], centerer[:], r[c], start=True, stop=True)
+            nc.tensor.matmul(mean[c], averager[:], r_bf[c], start=True, stop=True)
+        for c in chunks:
+            nc.vector.tensor_sub(dev[c], r[c], mean[c])
 
         inv_mag_root = per_chunk(F32, "inv_mag_root")
         inv_mag = per_chunk(F32, "inv_mag")

@@ -15,8 +15,6 @@ EPS = 1e-6
 TINY = 1e-30
 CHUNKS = 4
 CH = PIECE // CHUNKS
-QUARTER = S // 4
-WARM_UPS = 5
 
 FLOPS = 2 * P * P * N
 
@@ -33,8 +31,7 @@ def tile_ubercrsn_kernel(tc, table, w, ln_scale, ln_shift, focus_mask, mod_bias,
         offsets = held.tile([P, N // 16], U16, name="offsets")
         nc.sync.dma_start(offsets[:], offs)
         words = held.tile([P, S], BF16, name="words")
-        for q in range(4):
-            nc.scalar.dma_start(words[:, q * QUARTER : (q + 1) * QUARTER], table[:, q * QUARTER : (q + 1) * QUARTER])
+        nc.scalar.dma_start(words[:], table)
 
         padded = held.tile([P, 5 * D], BF16, name="padded")
         for stripe in (0, 2, 4):
@@ -57,8 +54,6 @@ def tile_ubercrsn_kernel(tc, table, w, ln_scale, ln_shift, focus_mask, mod_bias,
         nc.vector.memset(averager[:], 0.0)
         nc.vector.memset(averager[0:D, 0:D], 1.0 / D)
         nc.vector.memset(averager[D:P, D:P], 1.0 / D)
-        zeros = held.tile([P, PIECE], BF16, name="zeros")
-        nc.vector.memset(zeros[:], 0.0)
         eps = held.tile([P, 1], F32, name="eps")
         eps_squared = held.tile([P, 1], F32, name="eps_squared")
         tiny = held.tile([P, 1], F32, name="tiny")
@@ -67,12 +62,6 @@ def tile_ubercrsn_kernel(tc, table, w, ln_scale, ln_shift, focus_mask, mod_bias,
         nc.vector.memset(eps_squared[:], EPS * EPS)
         nc.vector.memset(tiny[:], TINY)
         nc.vector.memset(inv_e[:], math.exp(-1.0))
-
-        idle_product = psum.tile([P, PIECE], F32, name="idle_product")
-        for i in range(WARM_UPS):
-            nc.tensor.matmul(idle_product[:], averager[:], zeros[:], start=True, stop=True)
-        for q in range(3):
-            nc.tensor.matmul(idle_product[:], averager[:], words[:, q * QUARTER : q * QUARTER + PIECE], start=True, stop=True)
 
         exp_neg = held.tile([P, 1], F32, name="exp_neg")
         one_plus_exp = held.tile([P, 1], F32, name="one_plus_exp")

@@ -143,7 +143,7 @@ def tile_ubercrsn_kernel(tc, table, w, ln_scale, ln_shift, focus_mask, mod_bias,
         inv_mag_nrm = per_chunk(F32, "inv_mag_nrm")
         keep_over_mag = per_chunk(F32, "keep_over_mag")
         y_gated = [work.tile([P, 2, CH], F32, name=f"y_gated{c}") for c in chunks]
-        result = [work.tile([P, 2, CH], F32, name=f"result{c}") for c in chunks]
+        result = [[work.tile([P, 2 * CH], F32, name=f"result{pair}_{part}") for part in range(2)] for pair in range(CHUNKS // 2)]
         for c in chunks:
             nc.vector.scalar_tensor_tensor(scaled[c], dev[c], gain[:], rstd[c], ALU.mult, ALU.mult)
         for c in chunks:
@@ -161,12 +161,14 @@ def tile_ubercrsn_kernel(tc, table, w, ln_scale, ln_shift, focus_mask, mod_bias,
             nc.vector.scalar_tensor_tensor(
                 keep_over_mag[c], inv_mag_nrm[c], relu_bias[:], inv_mag[c], ALU.mult, ALU.add
             )
-        out_by_feature = out.rearrange("(part m) n -> m part n", part=2)
-        for c in chunks:
+        for pair in range(CHUNKS // 2):
             for part in range(2):
-                nc.vector.scalar_tensor_tensor(
-                    result[c][:, part, :], keep_over_mag[c], 0.0, y_gated[c][:, part, :], ALU.max, ALU.mult
-                )
-            for half in range(2):
-                to = slice(half * PIECE + c * CH, half * PIECE + (c + 1) * CH)
-                nc.sync.dma_start(out_by_feature[:, :, to], result[c][half * D : (half + 1) * D, :, :])
+                for side in range(2):
+                    c = 2 * pair + side
+                    nc.vector.scalar_tensor_tensor(
+                        result[pair][part][:, side * CH : (side + 1) * CH],
+                        keep_over_mag[c], 0.0, y_gated[c][:, part, :], ALU.max, ALU.mult,
+                    )
+                for half in range(2):
+                    to = slice(half * PIECE + 2 * pair * CH, half * PIECE + 2 * (pair + 1) * CH)
+                    nc.sync.dma_start(out[part * D : (part + 1) * D, to], result[pair][part][half * D : (half + 1) * D, :])

@@ -26,34 +26,39 @@ def tile_ubercrsn_kernel(tc, table, w, ln_scale, ln_shift, focus_mask, mod_bias,
         tc.tile_pool(name="work", bufs=1) as work,
         tc.psum_pool(name="psum", bufs=1) as psum,
     ):
-        focus = held.tile([P, 1], F32, name="focus")
-        nc.sync.dma_start(focus[:], focus_mask)
+        weights = held.tile([P, P], BF16, name="weights")
+        nc.sync.dma_start(weights[:], w)
         offsets = held.tile([P, N // 16], U16, name="offsets")
         nc.sync.dma_start(offsets[:], offs)
         words = held.tile([P, S], BF16, name="words")
         nc.scalar.dma_start(words[:], table)
 
-        padded = held.tile([P, 5 * D], BF16, name="padded")
-        for stripe in (0, 2, 4):
-            nc.gpsimd.memset(padded[:, stripe * D : (stripe + 1) * D], 0.0)
-        nc.sync.dma_start(padded[:, D : 2 * D], w[:, 0:D])
-        nc.sync.dma_start(padded[:, 3 * D : 4 * D], w[:, D : 2 * D])
-
+        focus = held.tile([P, 1], F32, name="focus")
         ln_gain = held.tile([P, 1], F32, name="ln_gain")
         ln_bias = held.tile([P, 1], F32, name="ln_bias")
         relu_bias = held.tile([P, 1], F32, name="relu_bias")
-        nc.sync.dma_start(ln_gain[:], ln_scale)
-        nc.sync.dma_start(ln_bias[:], ln_shift)
-        nc.sync.dma_start(relu_bias[:], mod_bias)
+        for vector, source in ((focus, focus_mask), (ln_gain, ln_scale), (ln_bias, ln_shift), (relu_bias, mod_bias)):
+            for half in range(2):
+                nc.sync.dma_start(vector[half:P:2, :], source[half * D : (half + 1) * D, :])
+
+        spread = held.tile([P, 2, 2, P], BF16, name="spread")
+        nc.vector.memset(spread[:], 0.0)
+        for part in range(2):
+            for half in range(2):
+                nc.vector.tensor_copy(spread[:, part, half, half:P:2], weights[:, part * D : (part + 1) * D])
 
         one = held.tile([P, 1], F32, name="one")
         nc.vector.memset(one[:], 1.0)
         first_use = held.tile([P, 1], F32, name="first_use")
         nc.scalar.activation(first_use[:], one[:], ACT.Abs_reciprocal_sqrt)
+        halves = held.tile([P, P], BF16, name="halves")
+        nc.vector.memset(halves[:], 0.0)
+        nc.vector.memset(halves[0:1, 0:P:2], 1.0)
+        nc.vector.memset(halves[32:33, 1:P:2], 1.0)
+        same_half = psum.tile([P, P], F32, name="same_half")
+        nc.tensor.matmul(same_half[:], halves[:], halves[:], start=True, stop=True)
         averager = held.tile([P, P], BF16, name="averager")
-        nc.vector.memset(averager[:], 0.0)
-        nc.vector.memset(averager[0:D, 0:D], 1.0 / D)
-        nc.vector.memset(averager[D:P, D:P], 1.0 / D)
+        nc.vector.tensor_scalar_mul(averager[:], same_half[:], 1.0 / D)
         eps = held.tile([P, 1], F32, name="eps")
         eps_squared = held.tile([P, 1], F32, name="eps_squared")
         tiny = held.tile([P, 1], F32, name="tiny")
@@ -78,10 +83,10 @@ def tile_ubercrsn_kernel(tc, table, w, ln_scale, ln_shift, focus_mask, mod_bias,
         second = words[:].indirect(offsets[:, PIECE // 16 : N // 16])
         real = psum.tile([P, PIECE], F32, name="real")
         imag = psum.tile([P, PIECE], F32, name="imag")
-        nc.tensor.matmul(real[:], padded[:, D : 3 * D], first, start=True, stop=False)
-        nc.tensor.matmul(real[:], padded[:, 0 : 2 * D], second, start=False, stop=True)
-        nc.tensor.matmul(imag[:], padded[:, 3 * D : 5 * D], first, start=True, stop=False)
-        nc.tensor.matmul(imag[:], padded[:, 2 * D : 4 * D], second, start=False, stop=True)
+        nc.tensor.matmul(real[:], spread[:, 0, 0, :], first, start=True, stop=False)
+        nc.tensor.matmul(real[:], spread[:, 0, 1, :], second, start=False, stop=True)
+        nc.tensor.matmul(imag[:], spread[:, 1, 0, :], first, start=True, stop=False)
+        nc.tensor.matmul(imag[:], spread[:, 1, 1, :], second, start=False, stop=True)
 
         chunks = range(CHUNKS)
         cols = [slice(c * CH, (c + 1) * CH) for c in chunks]
@@ -161,6 +166,7 @@ def tile_ubercrsn_kernel(tc, table, w, ln_scale, ln_shift, focus_mask, mod_bias,
             nc.vector.scalar_tensor_tensor(
                 keep_over_mag[c], inv_mag_nrm[c], relu_bias[:], inv_mag[c], ALU.mult, ALU.add
             )
+        out_by_partition = out.rearrange("(part m) (half n) -> part (m half) n", part=2, half=2)
         for pair in range(CHUNKS // 2):
             for part in range(2):
                 for side in range(2):
@@ -169,6 +175,4 @@ def tile_ubercrsn_kernel(tc, table, w, ln_scale, ln_shift, focus_mask, mod_bias,
                         result[pair][part][:, side * CH : (side + 1) * CH],
                         keep_over_mag[c], 0.0, y_gated[c][:, part, :], ALU.max, ALU.mult,
                     )
-                for half in range(2):
-                    to = slice(half * PIECE + 2 * pair * CH, half * PIECE + 2 * (pair + 1) * CH)
-                    nc.sync.dma_start(out[part * D : (part + 1) * D, to], result[pair][part][half * D : (half + 1) * D, :])
+                nc.sync.dma_start(out_by_partition[part, :, 2 * pair * CH : 2 * (pair + 1) * CH], result[pair][part][:])

@@ -16,6 +16,8 @@ TINY = 1e-30
 CHUNKS = 4
 CH = PIECE // CHUNKS
 
+SUM_BANKS = 5
+
 FLOPS = 2 * P * P * N
 
 
@@ -25,6 +27,7 @@ def tile_ubercrsn_kernel(tc, table, w, ln_scale, ln_shift, focus_mask, mod_bias,
         tc.tile_pool(name="held", bufs=1) as held,
         tc.tile_pool(name="work", bufs=1) as work,
         tc.psum_pool(name="psum", bufs=1) as psum,
+        tc.psum_pool(name="sums", bufs=SUM_BANKS) as sums,
     ):
         weights = held.tile([P, P], BF16, name="weights")
         nc.sync.dma_start(weights[:], w)
@@ -95,8 +98,7 @@ def tile_ubercrsn_kernel(tc, table, w, ln_scale, ln_shift, focus_mask, mod_bias,
             return [work.tile([P, CH], dtype, name=f"{name}{c}")[:] for c in chunks]
 
         def per_chunk_psum(name):
-            banks = [psum.tile([P, 2 * CH], F32, name=f"{name}{i}") for i in range(CHUNKS // 2)]
-            return [banks[c // 2][:, (c % 2) * CH : (c % 2 + 1) * CH] for c in chunks]
+            return [sums.tile([P, CH], F32, name=f"{name}{c}", tag="sum")[:] for c in chunks]
 
         re2 = per_chunk(F32, "re2")
         im2 = per_chunk(F32, "im2")

import math

import concourse.mybir as mybir

BF16, F32, U16 = mybir.dt.bfloat16, mybir.dt.float32, mybir.dt.uint16
ACT = mybir.ActivationFunctionType
ALU = mybir.AluOpType

P = 128
S = 4096
N = 1024
D = 64
PIECE = N // 2
EPS = 1e-6
TINY = 1e-30
CHUNKS = 4
CH = PIECE // CHUNKS

SUM_BANKS = 5

FLOPS = 2 * P * P * N


def tile_ubercrsn_kernel(tc, table, w, ln_scale, ln_shift, focus_mask, mod_bias, offs, out):
    nc = tc.nc
    with (
        tc.tile_pool(name="held", bufs=1) as held,
        tc.tile_pool(name="work", bufs=1) as work,
        tc.psum_pool(name="psum", bufs=1) as psum,
        tc.psum_pool(name="sums", bufs=SUM_BANKS) as sums,
    ):
        weights = held.tile([P, P], BF16, name="weights")
        nc.sync.dma_start(weights[:], w)
        offsets = held.tile([P, N // 16], U16, name="offsets")
        nc.sync.dma_start(offsets[:], offs)
        words = held.tile([P, S], BF16, name="words")
        nc.scalar.dma_start(words[:], table)

        focus = held.tile([P, 1], F32, name="focus")
        ln_gain = held.tile([P, 1], F32, name="ln_gain")
        ln_bias = held.tile([P, 1], F32, name="ln_bias")
        relu_bias = held.tile([P, 1], F32, name="relu_bias")
        for vector, source in ((focus, focus_mask), (ln_gain, ln_scale), (ln_bias, ln_shift), (relu_bias, mod_bias)):
            for half in range(2):
                nc.sync.dma_start(vector[half:P:2, :], source[half * D : (half + 1) * D, :])

        spread = held.tile([P, 2, 2, P], BF16, name="spread")
        nc.vector.memset(spread[:], 0.0)
        for part in range(2):
            for half in range(2):
                nc.vector.tensor_copy(spread[:, part, half, half:P:2], weights[:, part * D : (part + 1) * D])

        one = held.tile([P, 1], F32, name="one")
        nc.vector.memset(one[:], 1.0)
        first_use = held.tile([P, 1], F32, name="first_use")
        nc.scalar.activation(first_use[:], one[:], ACT.Abs_reciprocal_sqrt)
        halves = held.tile([P, P], BF16, name="halves")
        nc.vector.memset(halves[:], 0.0)
        nc.vector.memset(halves[0:1, 0:P:2], 1.0)
        nc.vector.memset(halves[32:33, 1:P:2], 1.0)
        same_half = psum.tile([P, P], F32, name="same_half")
        nc.tensor.matmul(same_half[:], halves[:], halves[:], start=True, stop=True)
        averager = held.tile([P, P], BF16, name="averager")
        nc.vector.tensor_scalar_mul(averager[:], same_half[:], 1.0 / D)
        eps = held.tile([P, 1], F32, name="eps")
        eps_squared = held.tile([P, 1], F32, name="eps_squared")
        tiny = held.tile([P, 1], F32, name="tiny")
        inv_e = held.tile([P, 1], F32, name="inv_e")
        nc.vector.memset(eps[:], EPS)
        nc.vector.memset(eps_squared[:], EPS * EPS)
        nc.vector.memset(tiny[:], TINY)
        nc.vector.memset(inv_e[:], math.exp(-1.0))

        exp_neg = held.tile([P, 1], F32, name="exp_neg")
        one_plus_exp = held.tile([P, 1], F32, name="one_plus_exp")
        gate = held.tile([P, 1], F32, name="gate")
        nc.gpsimd.tensor_tensor(exp_neg[:], inv_e[:], focus[:], ALU.pow)
        nc.vector.tensor_scalar_add(one_plus_exp[:], exp_neg[:], 1.0)
        nc.vector.reciprocal(gate[:], one_plus_exp[:])
        gain = held.tile([P, 1], F32, name="gain")
        shift = held.tile([P, 1], F32, name="shift")
        nc.vector.tensor_mul(gain[:], ln_gain[:], gate[:])
        nc.vector.tensor_mul(shift[:], ln_bias[:], gate[:])

        first = words[:].indirect(offsets[:, 0 : PIECE // 16])
        second = words[:].indirect(offsets[:, PIECE // 16 : N // 16])
        real = psum.tile([P, PIECE], F32, name="real")
        imag = psum.tile([P, PIECE], F32, name="imag")
        nc.tensor.matmul(real[:], spread[:, 0, 0, :], first, start=True, stop=False)
        nc.tensor.matmul(real[:], spread[:, 0, 1, :], second, start=False, stop=True)
        nc.tensor.matmul(imag[:], spread[:, 1, 0, :], first, start=True, stop=False)
        nc.tensor.matmul(imag[:], spread[:, 1, 1, :], second, start=False, stop=True)

        chunks = range(CHUNKS)
        cols = [slice(c * CH, (c + 1) * CH) for c in chunks]

        def per_chunk(dtype, name):
            return [work.tile([P, CH], dtype, name=f"{name}{c}")[:] for c in chunks]

        def per_chunk_psum(name):
            return [sums.tile([P, CH], F32, name=f"{name}{c}", tag="sum")[:] for c in chunks]

        re2 = per_chunk(F32, "re2")
        im2 = per_chunk(F32, "im2")
        r2 = per_chunk(F32, "r2")
        inv_r = per_chunk(F32, "inv_r")
        r_bf = per_chunk(BF16, "r_bf")
        r = per_chunk(F32, "r")
        for c in chunks:
            nc.scalar.activation(re2[c], real[:, cols[c]], ACT.Square)
        for c in chunks:
            nc.scalar.activation(im2[c], imag[:, cols[c]], ACT.Square)
        for c in chunks:
            nc.vector.tensor_add(r2[c], re2[c], im2[c])
        for c in chunks:
            nc.scalar.activation(inv_r[c], r2[c], ACT.Abs_reciprocal_sqrt, bias=tiny[:])
        for c in chunks:
            nc.vector.tensor_mul(r_bf[c], r2[c], inv_r[c])
        for c in chunks:
            nc.vector.tensor_mul(r[c], r2[c], inv_r[c])

        mean = per_chunk_psum("mean")
        dev = per_chunk(F32, "dev")
        for c in chunks:
            nc.tensor.matmul(mean[c], averager[:], r_bf[c], start=True, stop=True)
        for c in chunks:
            nc.vector.tensor_sub(dev[c], r[c], mean[c])

        inv_mag_root = per_chunk(F32, "inv_mag_root")
        inv_mag = per_chunk(F32, "inv_mag")
        for c in chunks:
            nc.scalar.activation(inv_mag_root[c], r[c], ACT.Abs_reciprocal_sqrt, bias=eps[:])
        for c in chunks:
            nc.vector.tensor_mul(inv_mag[c], inv_mag_root[c], inv_mag_root[c])

        dev2 = per_chunk(BF16, "dev2")
        mean_dev2 = per_chunk_psum("mean_dev2")
        rstd = per_chunk(F32, "rstd")
        for c in chunks:
            nc.scalar.activation(dev2[c], dev[c], ACT.Square)
        for c in chunks:
            nc.tensor.matmul(mean_dev2[c], averager[:], dev2[c], start=True, stop=True)
        for c in chunks:
            nc.scalar.activation(rstd[c], mean_dev2[c], ACT.Abs_reciprocal_sqrt, bias=eps[:], scale=D / (D - 1.0))

        scaled = per_chunk(F32, "scaled")
        gated_abs = per_chunk(F32, "gated_abs")
        mag_nrm = per_chunk(F32, "mag_nrm")
        inv_mag_nrm_root = per_chunk(F32, "inv_mag_nrm_root")
        inv_mag_nrm = per_chunk(F32, "inv_mag_nrm")
        keep_over_mag = per_chunk(F32, "keep_over_mag")
        y_gated = [work.tile([P, 2, CH], F32, name=f"y_gated{c}") for c in chunks]
        result = [[work.tile([P, 2 * CH], F32, name=f"result{pair}_{part}") for part in range(2)] for pair in range(CHUNKS // 2)]
        for c in chunks:
            nc.vector.scalar_tensor_tensor(scaled[c], dev[c], gain[:], rstd[c], ALU.mult, ALU.mult)
        for c in chunks:
            nc.scalar.activation(gated_abs[c], scaled[c], ACT.Abs, bias=shift[:])
        for c in chunks:
            nc.vector.scalar_tensor_tensor(mag_nrm[c], gated_abs[c], EPS, r[c], ALU.add, ALU.mult)
        for c in chunks:
            nc.scalar.activation(inv_mag_nrm_root[c], mag_nrm[c], ACT.Abs_reciprocal_sqrt, bias=eps_squared[:])
        for c in chunks:
            nc.scalar.activation(inv_mag_nrm[c], inv_mag_nrm_root[c], ACT.Square)
        for c in chunks:
            nc.vector.scalar_tensor_tensor(y_gated[c][:, 0, :], scaled[c], shift[:], real[:, cols[c]], ALU.add, ALU.mult)
            nc.vector.scalar_tensor_tensor(y_gated[c][:, 1, :], scaled[c], shift[:], imag[:, cols[c]], ALU.add, ALU.mult)
        for c in chunks:
            nc.vector.scalar_tensor_tensor(
                keep_over_mag[c], inv_mag_nrm[c], relu_bias[:], inv_mag[c], ALU.mult, ALU.add
            )
        out_by_partition = out.rearrange("(part m) (half n) -> part (m half) n", part=2, half=2)
        for pair in range(CHUNKS // 2):
            for part in range(2):
                for side in range(2):
                    c = 2 * pair + side
                    nc.vector.scalar_tensor_tensor(
                        result[pair][part][:, side * CH : (side + 1) * CH],
                        keep_over_mag[c], 0.0, y_gated[c][:, part, :], ALU.max, ALU.mult,
                    )
                nc.sync.dma_start(out_by_partition[part, :, 2 * pair * CH : 2 * (pair + 1) * CH], result[pair][part][:])
